import numpy as np
import ml_dtypes


def mxq(x, axis, fmt="e4m3"):
    dtype, down = {"e4m3": (ml_dtypes.float8_e4m3fn, 7), "e5m2": (ml_dtypes.float8_e5m2, 14)}[fmt]
    v = np.moveaxis(np.asarray(x, np.float32).astype(ml_dtypes.bfloat16).astype(np.float64), axis, -1)
    blocks = v.reshape(v.shape[:-1] + (-1, 32))
    amax = np.abs(blocks).max(-1, keepdims=True)
    byte = np.maximum(np.where(amax > 0, np.frexp(amax)[1] - 1 + 127, 0) - down, 1)
    scale = np.exp2(byte - 127.0)
    codes = (blocks / scale).astype(np.float32).astype(dtype).astype(np.float64)
    return np.moveaxis((codes * scale).reshape(v.shape), -1, axis)


WIDE = False


def mx_kscale(k, group=512):
    if not WIDE:
        return np.ones(k)
    levels = np.array([18, -18])
    if group != 512:
        return np.exp2(np.random.permutation(np.resize(levels, k // group))).repeat(group)
    if k % 512:
        return np.exp2(np.random.permutation(np.resize(levels, k // 32))).repeat(32)
    a = np.empty((k // 512, 16))
    for p in range(k // 512):
        a[p, :8] = np.random.permutation(np.resize(levels, 8))
        for g in range(8):
            far = levels[np.abs(levels - a[p, g]) >= 10]
            a[p, g + 8] = far[np.random.randint(len(far))]
    return np.exp2(a.ravel()).repeat(32)


BF16 = ml_dtypes.bfloat16


def bf(x):
    return np.asarray(x, np.float32).astype(BF16)


def f64(x):
    return np.asarray(x).astype(np.float64)


B, N, VD, QD, D, H, NG, P = 32, 32, 2048, 1024, 1024, 2, 20, 64
DH = D // H
T = B * N


def preact(out_t, out_w, out_b, self_feat):
    t = f64(out_t).reshape(T, H, D).swapaxes(0, 1)
    nb = t @ f64(out_w)
    return f64(self_feat) + nb.swapaxes(0, 1).reshape(B, N, D) + f64(out_b)


def setup_inputs():
    s = mx_kscale(T).reshape(B, N, 1)
    u = mx_kscale(D, group=128)
    t0 = bf(np.random.standard_normal((B, N, H, D)) * 0.7)
    w0 = bf(np.random.standard_normal((H, D, DH)) / np.sqrt(D))
    out_b = bf(np.random.standard_normal(D) * 0.3)
    self_feat = bf(np.random.standard_normal((B, N, D)) * 0.9)
    vis = bf(np.maximum(np.random.standard_normal((B, N, D)), 0.0))
    g = bf(4.0 * np.random.standard_normal((B, N, D)) * np.exp2(np.random.randint(-6, 1, (B, N, 1))) / s * u)
    z = preact(t0, w0, out_b, self_feat)
    return {"out_t": bf(f64(t0) * s[..., None]),
            "out_w": bf(f64(w0) / u.reshape(H, 1, DH)),
            "out_b": out_b,
            "self_feat": self_feat,
            "vis": vis,
            "z": np.asarray(z, np.float32),
            "grad_out": g}


def reference(out_t, out_w, out_b, self_feat, vis, z, grad_out):
    dz = np.where(f64(z) > 0.0, f64(grad_out), 0.0)
    dz = dz.reshape(T, H, DH).swapaxes(0, 1)
    x = f64(out_t).reshape(T, H, D).swapaxes(0, 1)
    dt = mxq(dz, 2, "e5m2") @ mxq(f64(out_w), 2, "e4m3").swapaxes(1, 2)
    dw = mxq(x, 1, "e4m3").swapaxes(1, 2) @ mxq(dz, 1, "e5m2")
    return dt.swapaxes(0, 1).reshape(B, N, H, D), dw

@@ -1,0 +1,243 @@
+from contextlib import ExitStack
+
+import concourse.mybir as mybir
+from concourse.masks import make_identity
+
+T, H, D, DH = 1024, 2, 1024, 512
+FLOPS = 4 * T * H * D * DH
+BYTES = 2 * T * H * D + 2 * H * D * DH + 4 * T * H * DH + 2 * T * H * DH + 4 * T * H * D + 4 * H * D * DH
+
+P = 128
+PACK = 4
+GROUP = P * PACK
+GROUPS = T // GROUP
+CHUNK = 512
+
+F32 = mybir.dt.float32
+BF16 = mybir.dt.bfloat16
+U32 = mybir.dt.uint32
+U8 = mybir.dt.uint8
+E4X4 = mybir.dt.float8_e4m3fn_x4
+E5X4 = mybir.dt.float8_e5m2_x4
+GT = mybir.AluOpType.is_gt
+MULT = mybir.AluOpType.mult
+
+
+def tile_implicitrelationencoder_pb_v_kernel(
+    tc, out_t, out_w, out_b, self_feat, vis, z, grad_out, out_0, out_1
+):
+    nc = tc.nc
+    x_rows = out_t.rearrange("b n h d -> (b n) (h d)")
+    z_rows = z.rearrange("b n d -> (b n) d")
+    g_rows = grad_out.rearrange("b n d -> (b n) d")
+    o0_rows = out_0.rearrange("b n h d -> (b n) (h d)")
+
+    def group_view(rows, g):
+        return rows[g * GROUP : (g + 1) * GROUP, :].rearrange("(p j) d -> p j d", j=PACK)
+
+    with ExitStack() as ctx:
+        keep = ctx.enter_context(tc.tile_pool(name="keep", bufs=1))
+        work = ctx.enter_context(tc.tile_pool(name="work", bufs=1))
+        psum = ctx.enter_context(tc.psum_pool(name="psum", bufs=1))
+
+        ident = keep.tile([P, P], F32, name="ident")
+        make_identity(nc, ident[:])
+
+        xq = keep.tile([P, GROUPS * H * 2, CHUNK], U32, name="xq", align_bytes=64)
+        xs = keep.tile([P, GROUPS * H * 2, CHUNK], U8, name="xs", align_bytes=64)
+        tq = keep.tile([P, GROUPS * H, CHUNK], U32, name="tq", align_bytes=64)
+        ts = keep.tile([P, GROUPS * H, CHUNK], U8, name="ts", align_bytes=64)
+        fq = keep.tile([P, GROUPS * H, CHUNK], U32, name="fq", align_bytes=64)
+        fs = keep.tile([P, GROUPS * H, CHUNK], U8, name="fs", align_bytes=64)
+        wq = keep.tile([P, H * 2, CHUNK], U32, name="wq", align_bytes=64)
+        ws = keep.tile([P, H * 2, CHUNK], U8, name="ws", align_bytes=64)
+
+        z_sb, g_sb, w_sb, x_sb, dz_sb = {}, {}, {}, {}, {}
+
+        def load_dz_inputs(g):
+            z_sb[g] = work.tile([P, PACK, H * DH], F32, name="zt", tag="k16", bufs=2)
+            g_sb[g] = work.tile([P, PACK, H * DH], BF16, name="gt", tag="k8", bufs=8)
+            for a in range(2):
+                js = slice(2 * a, 2 * a + 2)
+                nc.sync.dma_start(out=z_sb[g][:, js, :], in_=group_view(z_rows, g)[:, js, :])
+                nc.sync.dma_start(out=g_sb[g][:, js, :], in_=group_view(g_rows, g)[:, js, :])
+
+        def load_w(h):
+            w_sb[h] = work.tile([P, 2, 4 * DH], BF16, name="wt", tag="k8", bufs=8)
+            nc.sync.dma_start(
+                out=w_sb[h][:], in_=out_w[h].rearrange("(c q m) o -> q c (m o)", c=2, m=4)
+            )
+
+        def load_x(g):
+            x_sb[g] = work.tile([P, PACK, H * D], BF16, name="xt", tag="x16", bufs=2)
+            nc.sync.dma_start(out=x_sb[g][:], in_=group_view(x_rows, g))
+
+        def make_dz(g, a):
+            js = slice(2 * a, 2 * a + 2)
+            if a == 0:
+                dz_sb[g] = work.tile([P, PACK, H * DH], BF16, name="dzt", tag="dz", bufs=2, align_bytes=64)
+            nc.vector.scalar_tensor_tensor(
+                out=dz_sb[g][:, js, :], in0=z_sb[g][:, js, :], scalar=0.0,
+                in1=g_sb[g][:, js, :], op0=GT, op1=MULT,
+            )
+
+        fgrp = {}
+
+        def turn_dz(g, a):
+            grp = work.tile([P, 2048], BF16, name="fgrp", tag="grp", bufs=4, align_bytes=64)
+            fgrp[g, a] = grp
+            words = dz_sb[g][:].rearrange("p j w -> p (j w)").bitcast(F32)
+            for h in range(H):
+                tp = psum.tile([P, 4, P], F32, name="tp", tag="tp", bufs=3)
+                for jj in range(2):
+                    for u in range(2):
+                        off = (2 * a + jj) * 512 + h * 256
+                        nc.tensor.transpose(tp[:, 2 * jj + u, :], words[:, off + u : off + 256 : 2], ident[:])
+                nc.scalar.copy(
+                    out=grp[:].bitcast(F32)[:, h * 512 : (h + 1) * 512].rearrange("p (j r u) -> p j r u", j=2, u=2),
+                    in_=tp[:].rearrange("p (j u) r -> p j r u", u=2),
+                )
+
+        def quant_dz_feat(g, a, h):
+            cols = slice(a * 256, (a + 1) * 256)
+            nc.vector.quantize_mx(
+                out=fq[:, g * H + h, cols].bitcast(E5X4), scales=fs[:, g * H + h, cols],
+                in_=fgrp[g, a][:, h * 1024 : (h + 1) * 1024],
+            )
+
+        wgrp = {}
+
+        def turn_w(h, c):
+            grp = work.tile([P, 2048], BF16, name="wgrp", tag="grp", bufs=4, align_bytes=64)
+            wgrp[h, c] = grp
+            words = w_sb[h][:].rearrange("p c r -> p (c r)").bitcast(F32)
+            dst = grp[:].bitcast(F32).rearrange("p (q k) -> p q k", k=8)
+            for mm in range(2):
+                tp = psum.tile([P, 4, P], F32, name="tp", tag="tp", bufs=3)
+                for i in range(2):
+                    for u in range(2):
+                        off = c * 1024 + (2 * mm + i) * 256
+                        nc.tensor.transpose(tp[:, 2 * i + u, :], words[:, off + u : off + 256 : 2], ident[:])
+                nc.scalar.copy(out=dst[:, :, 4 * mm : 4 * mm + 4], in_=tp[:].rearrange("p k q -> p q k"))
+
+        def quant_w(h, c):
+            nc.vector.quantize_mx(out=wq[:, 2 * h + c, :].bitcast(E4X4), scales=ws[:, 2 * h + c, :], in_=wgrp[h, c][:])
+
+        tgrp = {}
+
+        def lay_dz_tok(g, h):
+            grp = work.tile([P, 2048], BF16, name="tgrp", tag="il", bufs=4, align_bytes=64)
+            tgrp[g, h] = grp
+            nc.vector.tensor_copy(
+                out=grp[:].rearrange("p (w j) -> p w j", j=PACK),
+                in_=dz_sb[g][:, :, h * DH : (h + 1) * DH].rearrange("p j w -> p w j"),
+            )
+
+        def quant_dz_tok(g, h):
+            nc.vector.quantize_mx(out=tq[:, g * H + h, :].bitcast(E5X4), scales=ts[:, g * H + h, :], in_=tgrp[g, h][:])
+
+        xgrp = {}
+
+        def lay_x(g, i):
+            grp = work.tile([P, 2048], BF16, name="xgrp", tag="il", bufs=4, align_bytes=64)
+            xgrp[g, i] = grp
+            nc.vector.tensor_copy(
+                out=grp[:].rearrange("p (m q j) -> p m q j", m=4, j=PACK),
+                in_=x_sb[g][:, :, i * CHUNK : (i + 1) * CHUNK].rearrange("p j (q m) -> p m q j", m=4),
+            )
+
+        def quant_x(g, i):
+            nc.vector.quantize_mx(out=xq[:, g * 4 + i, :].bitcast(E4X4), scales=xs[:, g * 4 + i, :], in_=xgrp[g, i][:])
+
+        def make_out0(g, j):
+            o0 = work.tile([P, H * D], F32, name="o0", tag="k8", bufs=8)
+            rows = slice(j * P, (j + 1) * P)
+            for h in range(H):
+                for c in range(2):
+                    acc = psum.tile([P, CHUNK], F32, name="acc", tag="acc", bufs=5)
+                    nc.tensor.matmul_mx(
+                        out=acc[:],
+                        lhsT=fq[:, g * H + h, rows].bitcast(E5X4), lhsT_scale=fs[:, g * H + h, rows],
+                        rhs=wq[:, 2 * h + c, :].bitcast(E4X4), rhs_scale=ws[:, 2 * h + c, :],
+                        start=True, stop=True,
+                    )
+                    nc.scalar.copy(out=o0[:, (2 * h + c) * CHUNK : (2 * h + c + 1) * CHUNK], in_=acc[:])
+            nc.sync.dma_start(out=group_view(o0_rows, g)[:, j, :], in_=o0[:])
+
+        o1_sb = {}
+
+        def make_out1(h, c):
+            if c == 0:
+                o1_sb[h] = work.tile([P, 2, 4, DH], F32, name="o1", tag="k16", bufs=2)
+            for m in range(4):
+                cols = slice(m * P, (m + 1) * P)
+                acc = psum.tile([P, CHUNK], F32, name="acc", tag="acc", bufs=5)
+                for g in range(GROUPS):
+                    nc.tensor.matmul_mx(
+                        out=acc[:],
+                        lhsT=xq[:, g * 4 + 2 * h + c, cols].bitcast(E4X4), lhsT_scale=xs[:, g * 4 + 2 * h + c, cols],
+                        rhs=tq[:, g * H + h, :].bitcast(E5X4), rhs_scale=ts[:, g * H + h, :],
+                        start=(g == 0), stop=(g == GROUPS - 1),
+                    )
+                if h == 1 and c == 1 and m % 2 == 1:
+                    nc.vector.tensor_copy(out=o1_sb[h][:, c, m, :], in_=acc[:])
+                else:
+                    nc.scalar.copy(out=o1_sb[h][:, c, m, :], in_=acc[:])
+            nc.sync.dma_start(
+                out=out_1[h].rearrange("(c q m) o -> c q (m o)", c=2, m=4)[c],
+                in_=o1_sb[h][:, c, :, :].rearrange("p m o -> p (m o)"),
+            )
+
+        with tc.manual_schedule():
+            load_dz_inputs(0)
+            load_w(0)
+            load_w(1)
+            load_dz_inputs(1)
+            load_x(0)
+            load_x(1)
+
+            make_dz(0, 0)
+            turn_dz(0, 0)
+            make_dz(0, 1)
+            turn_dz(0, 1)
+            lay_dz_tok(0, 0)
+            quant_dz_feat(0, 0, 0)
+            quant_dz_feat(0, 0, 1)
+            lay_dz_tok(0, 1)
+            quant_dz_tok(0, 0)
+            quant_dz_feat(0, 1, 0)
+            quant_dz_feat(0, 1, 1)
+            quant_dz_tok(0, 1)
+            for h in range(H):
+                for c in range(2):
+                    turn_w(h, c)
+            for h in range(H):
+                for c in range(2):
+                    quant_w(h, c)
+            make_dz(1, 0)
+            make_out0(0, 0)
+            turn_dz(1, 0)
+            make_out0(0, 1)
+            make_dz(1, 1)
+            turn_dz(1, 1)
+            lay_dz_tok(1, 0)
+            quant_dz_feat(1, 0, 0)
+            quant_dz_feat(1, 0, 1)
+            make_out0(0, 2)
+            lay_dz_tok(1, 1)
+            quant_dz_tok(1, 0)
+            quant_dz_feat(1, 1, 0)
+            quant_dz_feat(1, 1, 1)
+            make_out0(0, 3)
+            quant_dz_tok(1, 1)
+            order = [(g, i) for g in range(GROUPS) for i in range(4)]
+            for n in range(len(order)):
+                lay_x(*order[n])
+                if n > 0:
+                    quant_x(*order[n - 1])
+                if n < 4:
+                    make_out0(1, n)
+                if n > 4:
+                    make_out1((n - 5) // 2, (n - 5) % 2)
+            quant_x(*order[-1])
+            make_out1(1, 1)

@@ -10,6 +10,8 @@ BYTES = 2 * T * H * D + 2 * H * D * DH + 4 * T * H * DH + 2 * T * H * DH + 4 * T
 P = 128
 PACK = 4
 GROUP = P * PACK
+W = 2
+E = 4 // W
 GROUPS = T // GROUP
 CHUNK = 512
 
@@ -54,36 +56,43 @@ def tile_implicitrelationencoder_pb_v_kernel(
 
         z_sb, g_sb, w_sb, x_sb, dz_sb = {}, {}, {}, {}, {}
 
-        def load_dz_inputs(g):
-            z_sb[g] = work.tile([P, PACK, H * DH], F32, name="zt", tag="k16", bufs=2)
-            g_sb[g] = work.tile([P, PACK, H * DH], BF16, name="gt", tag="k8", bufs=8)
-            for a in range(2):
-                js = slice(2 * a, 2 * a + 2)
-                nc.sync.dma_start(out=z_sb[g][:, js, :], in_=group_view(z_rows, g)[:, js, :])
-                nc.sync.dma_start(out=g_sb[g][:, js, :], in_=group_view(g_rows, g)[:, js, :])
+        def open_group(g):
+            z_sb[g] = work.tile([P, PACK, H * DH], F32, name="zt", tag="k16", bufs=4)
+            g_sb[g] = work.tile([P, PACK, H * DH], BF16, name="gt", tag="g8", bufs=2)
+            dz_sb[g] = work.tile([P, PACK, H * DH], BF16, name="dzt", tag="dz", bufs=2, align_bytes=64)
 
-        def load_w(h):
-            w_sb[h] = work.tile([P, 2, 4 * DH], BF16, name="wt", tag="k8", bufs=8)
+        def load_dz_rows(g, lo, hi):
+            js = slice(lo, hi)
+            nc.sync.dma_start(out=z_sb[g][:, js, :], in_=group_view(z_rows, g)[:, js, :])
+            nc.sync.dma_start(out=g_sb[g][:, js, :], in_=group_view(g_rows, g)[:, js, :])
+
+        def load_w(h, c):
+            if c == 0:
+                w_sb[h] = work.tile([P, 2, 4 * DH], BF16, name="wt", tag="w8", bufs=2)
             nc.sync.dma_start(
-                out=w_sb[h][:], in_=out_w[h].rearrange("(c q m) o -> q c (m o)", c=2, m=4)
+                out=w_sb[h][:, c, :], in_=out_w[h].rearrange("(c q m) o -> c q (m o)", c=2, m=4)[c]
             )
 
         def load_x(g):
             x_sb[g] = work.tile([P, PACK, H * D], BF16, name="xt", tag="x16", bufs=2)
             nc.sync.dma_start(out=x_sb[g][:], in_=group_view(x_rows, g))
 
-        def make_dz(g, a):
-            js = slice(2 * a, 2 * a + 2)
-            if a == 0:
-                dz_sb[g] = work.tile([P, PACK, H * DH], BF16, name="dzt", tag="dz", bufs=2, align_bytes=64)
+        def make_dz(g, lo, hi):
+            js = slice(lo, hi)
             nc.vector.scalar_tensor_tensor(
                 out=dz_sb[g][:, js, :], in0=z_sb[g][:, js, :], scalar=0.0,
                 in1=g_sb[g][:, js, :], op0=GT, op1=MULT,
             )
 
+        def copy_on(engine, out, in_):
+            if engine == "v":
+                nc.vector.tensor_copy(out=out, in_=in_)
+            else:
+                nc.scalar.copy(out=out, in_=in_)
+
         fgrp = {}
 
-        def turn_dz(g, a):
+        def turn_dz(g, a, engines):
             grp = work.tile([P, 2048], BF16, name="fgrp", tag="grp", bufs=4, align_bytes=64)
             fgrp[g, a] = grp
             words = dz_sb[g][:].rearrange("p j w -> p (j w)").bitcast(F32)
@@ -93,7 +102,8 @@ def tile_implicitrelationencoder_pb_v_kernel(
                     for u in range(2):
                         off = (2 * a + jj) * 512 + h * 256
                         nc.tensor.transpose(tp[:, 2 * jj + u, :], words[:, off + u : off + 256 : 2], ident[:])
-                nc.scalar.copy(
+                copy_on(
+                    engines[h],
                     out=grp[:].bitcast(F32)[:, h * 512 : (h + 1) * 512].rearrange("p (j r u) -> p j r u", j=2, u=2),
                     in_=tp[:].rearrange("p (j u) r -> p j r u", u=2),
                 )
@@ -107,7 +117,7 @@ def tile_implicitrelationencoder_pb_v_kernel(
 
         wgrp = {}
 
-        def turn_w(h, c):
+        def turn_w(h, c, engines):
             grp = work.tile([P, 2048], BF16, name="wgrp", tag="grp", bufs=4, align_bytes=64)
             wgrp[h, c] = grp
             words = w_sb[h][:].rearrange("p c r -> p (c r)").bitcast(F32)
@@ -118,17 +128,18 @@ def tile_implicitrelationencoder_pb_v_kernel(
                     for u in range(2):
                         off = c * 1024 + (2 * mm + i) * 256
                         nc.tensor.transpose(tp[:, 2 * i + u, :], words[:, off + u : off + 256 : 2], ident[:])
-                nc.scalar.copy(out=dst[:, :, 4 * mm : 4 * mm + 4], in_=tp[:].rearrange("p k q -> p q k"))
+                copy_on(engines[mm], out=dst[:, :, 4 * mm : 4 * mm + 4], in_=tp[:].rearrange("p k q -> p q k"))
 
         def quant_w(h, c):
             nc.vector.quantize_mx(out=wq[:, 2 * h + c, :].bitcast(E4X4), scales=ws[:, 2 * h + c, :], in_=wgrp[h, c][:])
 
         tgrp = {}
 
-        def lay_dz_tok(g, h):
+        def lay_dz_tok(g, h, engine):
             grp = work.tile([P, 2048], BF16, name="tgrp", tag="il", bufs=4, align_bytes=64)
             tgrp[g, h] = grp
-            nc.vector.tensor_copy(
+            copy_on(
+                engine,
                 out=grp[:].rearrange("p (w j) -> p w j", j=PACK),
                 in_=dz_sb[g][:, :, h * DH : (h + 1) * DH].rearrange("p j w -> p w j"),
             )
@@ -138,19 +149,23 @@ def tile_implicitrelationencoder_pb_v_kernel(
 
         xgrp = {}
 
-        def lay_x(g, i):
+        def lay_x(g, i, engine):
             grp = work.tile([P, 2048], BF16, name="xgrp", tag="il", bufs=4, align_bytes=64)
             xgrp[g, i] = grp
-            nc.vector.tensor_copy(
-                out=grp[:].rearrange("p (m q j) -> p m q j", m=4, j=PACK),
-                in_=x_sb[g][:, :, i * CHUNK : (i + 1) * CHUNK].rearrange("p j (q m) -> p m q j", m=4),
+            copy_on(
+                engine,
+                out=grp[:].rearrange("p (m r j) -> p m r j", m=W, j=PACK),
+                in_=x_sb[g][:, :, i * CHUNK : (i + 1) * CHUNK].rearrange("p j (r m) -> p m r j", m=W),
             )
 
         def quant_x(g, i):
             nc.vector.quantize_mx(out=xq[:, g * 4 + i, :].bitcast(E4X4), scales=xs[:, g * 4 + i, :], in_=xgrp[g, i][:])
 
-        def make_out0(g, j):
-            o0 = work.tile([P, H * D], F32, name="o0", tag="k8", bufs=8)
+        o0_sb = {}
+
+        def make_out0(g, j, engines="ssss"):
+            if j % 2 == 0:
+                o0_sb[g] = work.tile([P, 2, H * D], F32, name="o0", tag="k16", bufs=4)
             rows = slice(j * P, (j + 1) * P)
             for h in range(H):
                 for c in range(2):
@@ -161,16 +176,20 @@ def tile_implicitrelationencoder_pb_v_kernel(
                         rhs=wq[:, 2 * h + c, :].bitcast(E4X4), rhs_scale=ws[:, 2 * h + c, :],
                         start=True, stop=True,
                     )
-                    nc.scalar.copy(out=o0[:, (2 * h + c) * CHUNK : (2 * h + c + 1) * CHUNK], in_=acc[:])
-            nc.sync.dma_start(out=group_view(o0_rows, g)[:, j, :], in_=o0[:])
+                    copy_on(
+                        engines[2 * h + c],
+                        out=o0_sb[g][:, j % 2, (2 * h + c) * CHUNK : (2 * h + c + 1) * CHUNK], in_=acc[:],
+                    )
+            nc.sync.dma_start(out=group_view(o0_rows, g)[:, j, :], in_=o0_sb[g][:, j % 2, :])
 
         o1_sb = {}
 
-        def make_out1(h, c):
+        def make_out1(h, c, engines):
             if c == 0:
-                o1_sb[h] = work.tile([P, 2, 4, DH], F32, name="o1", tag="k16", bufs=2)
-            for m in range(4):
-                cols = slice(m * P, (m + 1) * P)
+                o1_sb[h] = work.tile([P, 2, E, W * DH], F32, name="o1", tag="x16", bufs=2)
+            for i in range(4):
+                cols = slice(i * P, (i + 1) * P)
+                m, e = divmod(i, E)
                 acc = psum.tile([P, CHUNK], F32, name="acc", tag="acc", bufs=5)
                 for g in range(GROUPS):
                     nc.tensor.matmul_mx(
@@ -179,65 +198,82 @@ def tile_implicitrelationencoder_pb_v_kernel(
                         rhs=tq[:, g * H + h, :].bitcast(E5X4), rhs_scale=ts[:, g * H + h, :],
                         start=(g == 0), stop=(g == GROUPS - 1),
                     )
-                if h == 1 and c == 1 and m % 2 == 1:
-                    nc.vector.tensor_copy(out=o1_sb[h][:, c, m, :], in_=acc[:])
-                else:
-                    nc.scalar.copy(out=o1_sb[h][:, c, m, :], in_=acc[:])
+                copy_on(engines[i], out=o1_sb[h][:, c, e, m * DH : (m + 1) * DH], in_=acc[:])
             nc.sync.dma_start(
-                out=out_1[h].rearrange("(c q m) o -> c q (m o)", c=2, m=4)[c],
-                in_=o1_sb[h][:, c, :, :].rearrange("p m o -> p (m o)"),
+                out=out_1[h].rearrange("(c e q m) o -> c q e (m o)", c=2, e=E, m=W)[c],
+                in_=o1_sb[h][:, c, :, :],
             )
 
         with tc.manual_schedule():
-            load_dz_inputs(0)
-            load_w(0)
-            load_w(1)
-            load_dz_inputs(1)
+            open_group(0)
+            open_group(1)
+            load_dz_rows(0, 0, 2)
+            load_dz_rows(0, 2, 4)
+            load_w(0, 0)
+            load_w(0, 1)
+            load_dz_rows(1, 0, 2)
+            load_w(1, 0)
+            load_w(1, 1)
+            load_dz_rows(1, 2, 4)
             load_x(0)
             load_x(1)
-
-            make_dz(0, 0)
-            turn_dz(0, 0)
-            make_dz(0, 1)
-            turn_dz(0, 1)
-            lay_dz_tok(0, 0)
+            make_dz(0, 0, 2)
+            turn_dz(0, 0, "ss")
+            make_dz(0, 2, 4)
+            turn_dz(0, 1, "ss")
+            lay_dz_tok(0, 0, "v")
             quant_dz_feat(0, 0, 0)
             quant_dz_feat(0, 0, 1)
-            lay_dz_tok(0, 1)
+            lay_dz_tok(0, 1, "v")
             quant_dz_tok(0, 0)
             quant_dz_feat(0, 1, 0)
             quant_dz_feat(0, 1, 1)
+            turn_w(0, 0, "ss")
+            turn_w(0, 1, "ss")
+            quant_w(0, 0)
+            make_dz(1, 0, 2)
+            quant_w(0, 1)
             quant_dz_tok(0, 1)
-            for h in range(H):
-                for c in range(2):
-                    turn_w(h, c)
-            for h in range(H):
-                for c in range(2):
-                    quant_w(h, c)
-            make_dz(1, 0)
-            make_out0(0, 0)
-            turn_dz(1, 0)
-            make_out0(0, 1)
-            make_dz(1, 1)
-            turn_dz(1, 1)
-            lay_dz_tok(1, 0)
+            turn_w(1, 0, "ss")
+            turn_w(1, 1, "ss")
+            quant_w(1, 0)
+            quant_w(1, 1)
+            turn_dz(1, 0, "ss")
+            make_dz(1, 2, 4)
+            make_out0(0, 0, "ssss")
+            make_out0(0, 1, "ssss")
+            turn_dz(1, 1, "ss")
+            lay_dz_tok(1, 0, "v")
             quant_dz_feat(1, 0, 0)
             quant_dz_feat(1, 0, 1)
-            make_out0(0, 2)
-            lay_dz_tok(1, 1)
+            make_out0(0, 2, "ssss")
+            lay_dz_tok(1, 1, "v")
             quant_dz_tok(1, 0)
             quant_dz_feat(1, 1, 0)
             quant_dz_feat(1, 1, 1)
-            make_out0(0, 3)
+            make_out0(0, 3, "ssss")
+            lay_x(0, 0, "v")
             quant_dz_tok(1, 1)
-            order = [(g, i) for g in range(GROUPS) for i in range(4)]
-            for n in range(len(order)):
-                lay_x(*order[n])
-                if n > 0:
-                    quant_x(*order[n - 1])
-                if n < 4:
-                    make_out0(1, n)
-                if n > 4:
-                    make_out1((n - 5) // 2, (n - 5) % 2)
-            quant_x(*order[-1])
-            make_out1(1, 1)
+            make_out0(1, 0, "ssss")
+            lay_x(0, 1, "v")
+            quant_x(0, 0)
+            make_out0(1, 1, "ssss")
+            lay_x(0, 2, "v")
+            quant_x(0, 1)
+            make_out0(1, 2, "ssss")
+            lay_x(0, 3, "v")
+            quant_x(0, 2)
+            make_out0(1, 3, "ssss")
+            lay_x(1, 0, "v")
+            quant_x(0, 3)
+            lay_x(1, 1, "v")
+            quant_x(1, 0)
+            make_out1(0, 0, "ssss")
+            lay_x(1, 2, "v")
+            quant_x(1, 1)
+            make_out1(0, 1, "ssss")
+            lay_x(1, 3, "v")
+            quant_x(1, 2)
+            make_out1(1, 0, "ssss")
+            quant_x(1, 3)
+            make_out1(1, 1, "svsv")

@@ -10,7 +10,7 @@ BYTES = 2 * T * H * D + 2 * H * D * DH + 4 * T * H * DH + 2 * T * H * DH + 4 * T
 P = 128
 PACK = 4
 GROUP = P * PACK
-W = 2
+W = 1
 E = 4 // W
 GROUPS = T // GROUP
 CHUNK = 512
@@ -140,8 +140,8 @@ def tile_implicitrelationencoder_pb_v_kernel(
             tgrp[g, h] = grp
             copy_on(
                 engine,
-                out=grp[:].rearrange("p (w j) -> p w j", j=PACK),
-                in_=dz_sb[g][:, :, h * DH : (h + 1) * DH].rearrange("p j w -> p w j"),
+                out=grp[:].rearrange("p (c i j) -> p c j i", i=4, j=PACK),
+                in_=dz_sb[g][:, :, h * DH : (h + 1) * DH].rearrange("p j (c i) -> p c j i", i=4),
             )
 
         def quant_dz_tok(g, h):
@@ -154,8 +154,8 @@ def tile_implicitrelationencoder_pb_v_kernel(
             xgrp[g, i] = grp
             copy_on(
                 engine,
-                out=grp[:].rearrange("p (m r j) -> p m r j", m=W, j=PACK),
-                in_=x_sb[g][:, :, i * CHUNK : (i + 1) * CHUNK].rearrange("p j (r m) -> p m r j", m=W),
+                out=grp[:].rearrange("p (c i j) -> p c j i", i=4, j=PACK),
+                in_=x_sb[g][:, :, i * CHUNK : (i + 1) * CHUNK].rearrange("p j (c i) -> p c j i", i=4),
             )
 
         def quant_x(g, i):

@@ -163,6 +163,13 @@ def tile_implicitrelationencoder_pb_v_kernel(
 
         o0_sb = {}
 
+        pending = []
+
+        def flush():
+            for dst, src in pending:
+                nc.scalar.dma_start(out=dst, in_=src)
+            pending.clear()
+
         def make_out0(g, j, engines="ssss"):
             if j % 2 == 0:
                 o0_sb[g] = work.tile([P, 2, H * D], F32, name="o0", tag="k16", bufs=4)
@@ -180,7 +187,12 @@ def tile_implicitrelationencoder_pb_v_kernel(
                         engines[2 * h + c],
                         out=o0_sb[g][:, j % 2, (2 * h + c) * CHUNK : (2 * h + c + 1) * CHUNK], in_=acc[:],
                     )
-            nc.sync.dma_start(out=group_view(o0_rows, g)[:, j, :], in_=o0_sb[g][:, j % 2, :])
+                    if h == 0 and c == 1:
+                        flush()
+            if j % 2 == 0:
+                nc.sync.dma_start(out=group_view(o0_rows, g)[:, j, :], in_=o0_sb[g][:, j % 2, :])
+            else:
+                pending.append((group_view(o0_rows, g)[:, j, :], o0_sb[g][:, j % 2, :]))
 
         o1_sb = {}
 
@@ -199,10 +211,16 @@ def tile_implicitrelationencoder_pb_v_kernel(
                         start=(g == 0), stop=(g == GROUPS - 1),
                     )
                 copy_on(engines[i], out=o1_sb[h][:, c, e, m * DH : (m + 1) * DH], in_=acc[:])
-            nc.sync.dma_start(
-                out=out_1[h].rearrange("(c e q m) o -> c q e (m o)", c=2, e=E, m=W)[c],
-                in_=o1_sb[h][:, c, :, :],
-            )
+                if i == 1:
+                    flush()
+            view = out_1[h].rearrange("(c e q m) o -> c q e (m o)", c=2, e=E, m=W)[c]
+            if (h, c) == (1, 1):
+                nc.sync.dma_start(out=view[:, 0:2, :], in_=o1_sb[h][:, c, 0:2, :])
+                nc.scalar.dma_start(out=view[:, 2:4, :], in_=o1_sb[h][:, c, 2:4, :])
+            elif c == 0:
+                nc.sync.dma_start(out=view, in_=o1_sb[h][:, c, :, :])
+            else:
+                pending.append((view, o1_sb[h][:, c, :, :]))
 
         with tc.manual_schedule():
             open_group(0)

from contextlib import ExitStack

import concourse.mybir as mybir
from concourse.masks import make_identity

T, H, D, DH = 1024, 2, 1024, 512
FLOPS = 4 * T * H * D * DH
BYTES = 2 * T * H * D + 2 * H * D * DH + 4 * T * H * DH + 2 * T * H * DH + 4 * T * H * D + 4 * H * D * DH

P = 128
PACK = 4
GROUP = P * PACK
W = 1
E = 4 // W
GROUPS = T // GROUP
CHUNK = 512

F32 = mybir.dt.float32
BF16 = mybir.dt.bfloat16
U32 = mybir.dt.uint32
U8 = mybir.dt.uint8
E4X4 = mybir.dt.float8_e4m3fn_x4
E5X4 = mybir.dt.float8_e5m2_x4
GT = mybir.AluOpType.is_gt
MULT = mybir.AluOpType.mult


def tile_implicitrelationencoder_pb_v_kernel(
    tc, out_t, out_w, out_b, self_feat, vis, z, grad_out, out_0, out_1
):
    nc = tc.nc
    x_rows = out_t.rearrange("b n h d -> (b n) (h d)")
    z_rows = z.rearrange("b n d -> (b n) d")
    g_rows = grad_out.rearrange("b n d -> (b n) d")
    o0_rows = out_0.rearrange("b n h d -> (b n) (h d)")

    def group_view(rows, g):
        return rows[g * GROUP : (g + 1) * GROUP, :].rearrange("(p j) d -> p j d", j=PACK)

    with ExitStack() as ctx:
        keep = ctx.enter_context(tc.tile_pool(name="keep", bufs=1))
        work = ctx.enter_context(tc.tile_pool(name="work", bufs=1))
        psum = ctx.enter_context(tc.psum_pool(name="psum", bufs=1))

        ident = keep.tile([P, P], F32, name="ident")
        make_identity(nc, ident[:])

        xq = keep.tile([P, GROUPS * H * 2, CHUNK], U32, name="xq", align_bytes=64)
        xs = keep.tile([P, GROUPS * H * 2, CHUNK], U8, name="xs", align_bytes=64)
        tq = keep.tile([P, GROUPS * H, CHUNK], U32, name="tq", align_bytes=64)
        ts = keep.tile([P, GROUPS * H, CHUNK], U8, name="ts", align_bytes=64)
        fq = keep.tile([P, GROUPS * H, CHUNK], U32, name="fq", align_bytes=64)
        fs = keep.tile([P, GROUPS * H, CHUNK], U8, name="fs", align_bytes=64)
        wq = keep.tile([P, H * 2, CHUNK], U32, name="wq", align_bytes=64)
        ws = keep.tile([P, H * 2, CHUNK], U8, name="ws", align_bytes=64)

        z_sb, g_sb, w_sb, x_sb, dz_sb = {}, {}, {}, {}, {}

        def open_group(g):
            z_sb[g] = work.tile([P, PACK, H * DH], F32, name="zt", tag="k16", bufs=4)
            g_sb[g] = work.tile([P, PACK, H * DH], BF16, name="gt", tag="g8", bufs=2)
            dz_sb[g] = work.tile([P, PACK, H * DH], BF16, name="dzt", tag="dz", bufs=2, align_bytes=64)

        def load_dz_rows(g, lo, hi):
            js = slice(lo, hi)
            nc.sync.dma_start(out=z_sb[g][:, js, :], in_=group_view(z_rows, g)[:, js, :])
            nc.sync.dma_start(out=g_sb[g][:, js, :], in_=group_view(g_rows, g)[:, js, :])

        def load_w(h, c):
            if c == 0:
                w_sb[h] = work.tile([P, 2, 4 * DH], BF16, name="wt", tag="w8", bufs=2)
            nc.sync.dma_start(
                out=w_sb[h][:, c, :], in_=out_w[h].rearrange("(c q m) o -> c q (m o)", c=2, m=4)[c]
            )

        def load_x(g):
            x_sb[g] = work.tile([P, PACK, H * D], BF16, name="xt", tag="x16", bufs=2)
            nc.sync.dma_start(out=x_sb[g][:], in_=group_view(x_rows, g))

        def make_dz(g, lo, hi):
            js = slice(lo, hi)
            nc.vector.scalar_tensor_tensor(
                out=dz_sb[g][:, js, :], in0=z_sb[g][:, js, :], scalar=0.0,
                in1=g_sb[g][:, js, :], op0=GT, op1=MULT,
            )

        def copy_on(engine, out, in_):
            if engine == "v":
                nc.vector.tensor_copy(out=out, in_=in_)
            else:
                nc.scalar.copy(out=out, in_=in_)

        fgrp = {}

        def turn_dz(g, a, engines):
            grp = work.tile([P, 2048], BF16, name="fgrp", tag="grp", bufs=4, align_bytes=64)
            fgrp[g, a] = grp
            words = dz_sb[g][:].rearrange("p j w -> p (j w)").bitcast(F32)
            for h in range(H):
                tp = psum.tile([P, 4, P], F32, name="tp", tag="tp", bufs=3)
                for jj in range(2):
                    for u in range(2):
                        off = (2 * a + jj) * 512 + h * 256
                        nc.tensor.transpose(tp[:, 2 * jj + u, :], words[:, off + u : off + 256 : 2], ident[:])
                copy_on(
                    engines[h],
                    out=grp[:].bitcast(F32)[:, h * 512 : (h + 1) * 512].rearrange("p (j r u) -> p j r u", j=2, u=2),
                    in_=tp[:].rearrange("p (j u) r -> p j r u", u=2),
                )

        def quant_dz_feat(g, a, h):
            cols = slice(a * 256, (a + 1) * 256)
            nc.vector.quantize_mx(
                out=fq[:, g * H + h, cols].bitcast(E5X4), scales=fs[:, g * H + h, cols],
                in_=fgrp[g, a][:, h * 1024 : (h + 1) * 1024],
            )

        wgrp = {}

        def turn_w(h, c, engines):
            grp = work.tile([P, 2048], BF16, name="wgrp", tag="grp", bufs=4, align_bytes=64)
            wgrp[h, c] = grp
            words = w_sb[h][:].rearrange("p c r -> p (c r)").bitcast(F32)
            dst = grp[:].bitcast(F32).rearrange("p (q k) -> p q k", k=8)
            for mm in range(2):
                tp = psum.tile([P, 4, P], F32, name="tp", tag="tp", bufs=3)
                for i in range(2):
                    for u in range(2):
                        off = c * 1024 + (2 * mm + i) * 256
                        nc.tensor.transpose(tp[:, 2 * i + u, :], words[:, off + u : off + 256 : 2], ident[:])
                copy_on(engines[mm], out=dst[:, :, 4 * mm : 4 * mm + 4], in_=tp[:].rearrange("p k q -> p q k"))

        def quant_w(h, c):
            nc.vector.quantize_mx(out=wq[:, 2 * h + c, :].bitcast(E4X4), scales=ws[:, 2 * h + c, :], in_=wgrp[h, c][:])

        tgrp = {}

        def lay_dz_tok(g, h, engine):
            grp = work.tile([P, 2048], BF16, name="tgrp", tag="il", bufs=4, align_bytes=64)
            tgrp[g, h] = grp
            copy_on(
                engine,
                out=grp[:].rearrange("p (c i j) -> p c j i", i=4, j=PACK),
                in_=dz_sb[g][:, :, h * DH : (h + 1) * DH].rearrange("p j (c i) -> p c j i", i=4),
            )

        def quant_dz_tok(g, h):
            nc.vector.quantize_mx(out=tq[:, g * H + h, :].bitcast(E5X4), scales=ts[:, g * H + h, :], in_=tgrp[g, h][:])

        xgrp = {}

        def lay_x(g, i, engine):
            grp = work.tile([P, 2048], BF16, name="xgrp", tag="il", bufs=4, align_bytes=64)
            xgrp[g, i] = grp
            copy_on(
                engine,
                out=grp[:].rearrange("p (c i j) -> p c j i", i=4, j=PACK),
                in_=x_sb[g][:, :, i * CHUNK : (i + 1) * CHUNK].rearrange("p j (c i) -> p c j i", i=4),
            )

        def quant_x(g, i):
            nc.vector.quantize_mx(out=xq[:, g * 4 + i, :].bitcast(E4X4), scales=xs[:, g * 4 + i, :], in_=xgrp[g, i][:])

        o0_sb = {}

        pending = []

        def flush():
            for dst, src in pending:
                nc.scalar.dma_start(out=dst, in_=src)
            pending.clear()

        def make_out0(g, j, engines="ssss"):
            if j % 2 == 0:
                o0_sb[g] = work.tile([P, 2, H * D], F32, name="o0", tag="k16", bufs=4)
            rows = slice(j * P, (j + 1) * P)
            for h in range(H):
                for c in range(2):
                    acc = psum.tile([P, CHUNK], F32, name="acc", tag="acc", bufs=5)
                    nc.tensor.matmul_mx(
                        out=acc[:],
                        lhsT=fq[:, g * H + h, rows].bitcast(E5X4), lhsT_scale=fs[:, g * H + h, rows],
                        rhs=wq[:, 2 * h + c, :].bitcast(E4X4), rhs_scale=ws[:, 2 * h + c, :],
                        start=True, stop=True,
                    )
                    copy_on(
                        engines[2 * h + c],
                        out=o0_sb[g][:, j % 2, (2 * h + c) * CHUNK : (2 * h + c + 1) * CHUNK], in_=acc[:],
                    )
                    if h == 0 and c == 1:
                        flush()
            if j % 2 == 0:
                nc.sync.dma_start(out=group_view(o0_rows, g)[:, j, :], in_=o0_sb[g][:, j % 2, :])
            else:
                pending.append((group_view(o0_rows, g)[:, j, :], o0_sb[g][:, j % 2, :]))

        o1_sb = {}

        def make_out1(h, c, engines):
            if c == 0:
                o1_sb[h] = work.tile([P, 2, E, W * DH], F32, name="o1", tag="x16", bufs=2)
            for i in range(4):
                cols = slice(i * P, (i + 1) * P)
                m, e = divmod(i, E)
                acc = psum.tile([P, CHUNK], F32, name="acc", tag="acc", bufs=5)
                for g in range(GROUPS):
                    nc.tensor.matmul_mx(
                        out=acc[:],
                        lhsT=xq[:, g * 4 + 2 * h + c, cols].bitcast(E4X4), lhsT_scale=xs[:, g * 4 + 2 * h + c, cols],
                        rhs=tq[:, g * H + h, :].bitcast(E5X4), rhs_scale=ts[:, g * H + h, :],
                        start=(g == 0), stop=(g == GROUPS - 1),
                    )
                copy_on(engines[i], out=o1_sb[h][:, c, e, m * DH : (m + 1) * DH], in_=acc[:])
                if i == 1:
                    flush()
            view = out_1[h].rearrange("(c e q m) o -> c q e (m o)", c=2, e=E, m=W)[c]
            if (h, c) == (1, 1):
                nc.sync.dma_start(out=view[:, 0:2, :], in_=o1_sb[h][:, c, 0:2, :])
                nc.scalar.dma_start(out=view[:, 2:4, :], in_=o1_sb[h][:, c, 2:4, :])
            elif c == 0:
                nc.sync.dma_start(out=view, in_=o1_sb[h][:, c, :, :])
            else:
                pending.append((view, o1_sb[h][:, c, :, :]))

        with tc.manual_schedule():
            open_group(0)
            open_group(1)
            load_dz_rows(0, 0, 2)
            load_dz_rows(0, 2, 4)
            load_w(0, 0)
            load_w(0, 1)
            load_dz_rows(1, 0, 2)
            load_w(1, 0)
            load_w(1, 1)
            load_dz_rows(1, 2, 4)
            load_x(0)
            load_x(1)
            make_dz(0, 0, 2)
            turn_dz(0, 0, "ss")
            make_dz(0, 2, 4)
            turn_dz(0, 1, "ss")
            lay_dz_tok(0, 0, "v")
            quant_dz_feat(0, 0, 0)
            quant_dz_feat(0, 0, 1)
            lay_dz_tok(0, 1, "v")
            quant_dz_tok(0, 0)
            quant_dz_feat(0, 1, 0)
            quant_dz_feat(0, 1, 1)
            turn_w(0, 0, "ss")
            turn_w(0, 1, "ss")
            quant_w(0, 0)
            make_dz(1, 0, 2)
            quant_w(0, 1)
            quant_dz_tok(0, 1)
            turn_w(1, 0, "ss")
            turn_w(1, 1, "ss")
            quant_w(1, 0)
            quant_w(1, 1)
            turn_dz(1, 0, "ss")
            make_dz(1, 2, 4)
            make_out0(0, 0, "ssss")
            make_out0(0, 1, "ssss")
            turn_dz(1, 1, "ss")
            lay_dz_tok(1, 0, "v")
            quant_dz_feat(1, 0, 0)
            quant_dz_feat(1, 0, 1)
            make_out0(0, 2, "ssss")
            lay_dz_tok(1, 1, "v")
            quant_dz_tok(1, 0)
            quant_dz_feat(1, 1, 0)
            quant_dz_feat(1, 1, 1)
            make_out0(0, 3, "ssss")
            lay_x(0, 0, "v")
            quant_dz_tok(1, 1)
            make_out0(1, 0, "ssss")
            lay_x(0, 1, "v")
            quant_x(0, 0)
            make_out0(1, 1, "ssss")
            lay_x(0, 2, "v")
            quant_x(0, 1)
            make_out0(1, 2, "ssss")
            lay_x(0, 3, "v")
            quant_x(0, 2)
            make_out0(1, 3, "ssss")
            lay_x(1, 0, "v")
            quant_x(0, 3)
            lay_x(1, 1, "v")
            quant_x(1, 0)
            make_out1(0, 0, "ssss")
            lay_x(1, 2, "v")
            quant_x(1, 1)
            make_out1(0, 1, "ssss")
            lay_x(1, 3, "v")
            quant_x(1, 2)
            make_out1(1, 0, "ssss")
            quant_x(1, 3)
            make_out1(1, 1, "svsv")
